import numpy as np
import ml_dtypes


def mxq(x, axis, fmt="e4m3"):
    dtype, down = {"e4m3": (ml_dtypes.float8_e4m3fn, 7), "e5m2": (ml_dtypes.float8_e5m2, 14)}[fmt]
    v = np.moveaxis(np.asarray(x, np.float32).astype(ml_dtypes.bfloat16).astype(np.float64), axis, -1)
    blocks = v.reshape(v.shape[:-1] + (-1, 32))
    amax = np.abs(blocks).max(-1, keepdims=True)
    byte = np.maximum(np.where(amax > 0, np.frexp(amax)[1] - 1 + 127, 0) - down, 1)
    scale = np.exp2(byte - 127.0)
    codes = (blocks / scale).astype(np.float32).astype(dtype).astype(np.float64)
    return np.moveaxis((codes * scale).reshape(v.shape), -1, axis)


WIDE = False


def mx_kscale(k):
    if not WIDE:
        return np.ones(k)
    levels = np.array([10, -10, 5, -5, 0])
    a = np.random.permutation(np.resize(levels, k // 512 * 4)).reshape(k // 512, 4)
    idx = np.arange(k)
    return np.exp2(a[idx // 512, idx % 128 // 32])


BF16 = ml_dtypes.bfloat16


def bf(x):
    return np.asarray(x, np.float32).astype(BF16)


def f64(x):
    return np.asarray(x).astype(np.float64)


B, L, H = 4, 2048, 512
HH = H // 2
BASE = 10000.0


def rope_tables():
    inv_freq = 1.0 / BASE ** (np.arange(0, H, 2) / H)
    freqs = np.outer(np.arange(L), inv_freq)
    emb = np.concatenate([freqs, freqs], axis=-1)
    return np.cos(emb), np.sin(emb)


def rotate_half(x):
    x1, x2 = np.split(x, 2, axis=-1)
    return np.concatenate([-x2, x1], axis=-1)


def setup_inputs():
    sh = mx_kscale(H)[:HH]
    s = np.concatenate([sh, sh])
    cos, sin = rope_tables()
    return {"hidden_states": bf(np.random.standard_normal((B, L, H)) * 0.2 * s),
            "W_q": bf(np.random.standard_normal((H, H)) * 0.5 / np.sqrt(H) / s[None, :]),
            "cos": bf(cos), "sin": bf(sin)}


def reference(hidden_states, W_q, cos, sin):
    x = f64(hidden_states)
    h = x * f64(cos)[None, :, :] + rotate_half(x) * f64(sin)[None, :, :]
    return mxq(h, 2, "e4m3") @ mxq(f64(W_q), 1, "e4m3").T

@@ -1,0 +1,183 @@
+from contextlib import ExitStack
+
+import concourse.mybir as mybir
+from concourse.masks import make_identity
+
+FP8X4 = mybir.dt.float8_e4m3fn_x4
+BF16 = mybir.dt.bfloat16
+F32 = mybir.dt.float32
+U32 = mybir.dt.uint32
+U8 = mybir.dt.uint8
+MULT = mybir.AluOpType.mult
+
+B, L, H = 4, 2048, 512
+HH = H // 2
+P = 128
+R = L // P
+KT = H // P
+FLOPS = 2 * B * L * H * H + 3 * B * L * H
+
+LOAD_CHUNKS = [1, 1, 2, 4, 4, 4]
+STORE_R = 2
+
+
+def tile_denseattentiononehead_pa_t_kernel(tc, hidden_states, W_q, cos, sin, out):
+    nc = tc.nc
+    x_v = hidden_states.rearrange("b (p r) j -> p b r j", r=R)
+    cos_v = cos.rearrange("(p r) j -> p r j", r=R)
+    sin_v = sin.rearrange("(p r) j -> p r j", r=R)
+    out_v = out.rearrange("b (p r) o -> p b r o", r=R)
+
+    with ExitStack() as ctx:
+        const = ctx.enter_context(tc.tile_pool(name="const", bufs=1))
+        resident = ctx.enter_context(tc.tile_pool(name="resident", bufs=1))
+        prod_pool = ctx.enter_context(tc.tile_pool(name="prod", bufs=2))
+        grp_pool = ctx.enter_context(tc.tile_pool(name="grp", bufs=2))
+        code_pool = ctx.enter_context(tc.tile_pool(name="code", bufs=2))
+        ost_pool = ctx.enter_context(tc.tile_pool(name="ost", bufs=3))
+        psum_h = ctx.enter_context(tc.psum_pool(name="psum_h", bufs=4))
+        psum_o = ctx.enter_context(tc.psum_pool(name="psum_o", bufs=4))
+        ctx.enter_context(tc.manual_schedule())
+
+        x_of = {}
+        tab_of = {}
+        first_of_chunk = {}
+        w_sb = const.tile([P, KT, H], BF16, name="w_sb")
+        r0 = 0
+        for c, rr in enumerate(LOAD_CHUNKS):
+            xt = resident.tile([P, B, rr, H], BF16, name="x%d" % c)
+            tab = resident.tile([P, 2, rr, H], BF16, name="tab%d" % c)
+            nc.sync.dma_start(out=xt[:], in_=x_v[:, :, r0 : r0 + rr, :])
+            nc.sync.dma_start(out=tab[:, 0, :, :], in_=cos_v[:, r0 : r0 + rr, :])
+            nc.sync.dma_start(out=tab[:, 1, :, 0:HH], in_=sin_v[:, r0 : r0 + rr, HH:H])
+            nc.sync.dma_start(out=tab[:, 1, :, HH:H], in_=sin_v[:, r0 : r0 + rr, 0:HH])
+            if c == 0:
+                nc.sync.dma_start(out=w_sb[:], in_=W_q.rearrange("(ob p) j -> p ob j", p=P))
+            first_of_chunk[r0] = tab
+            for rl in range(rr):
+                x_of[r0 + rl] = (xt, rl)
+                tab_of[r0 + rl] = (tab, rl)
+            r0 += rr
+
+        ident_f = const.tile([P, P], F32, name="ident_f")
+        make_identity(nc, ident_f[:])
+        ident_b = const.tile([P, P], BF16, name="ident_b")
+        make_identity(nc, ident_b[:])
+
+        w_grouped = const.tile([P, H, KT], BF16, name="w_grouped", align_bytes=64)
+        w_codes = const.tile([P, H], U32, name="w_codes", align_bytes=64)
+        w_scales = const.tile([P, H], U8, name="w_scales", align_bytes=64)
+
+        def prepare_w_transposes():
+            for half in range(2):
+                wt = psum_o.tile([P, KT, 2 * P], BF16, name="wt", tag="acc")
+                for t in range(KT):
+                    for o2 in range(2):
+                        nc.tensor.transpose(
+                            wt[:, t, o2 * P : (o2 + 1) * P],
+                            w_sb[:, 2 * half + o2, t * P : (t + 1) * P],
+                            ident_b[:],
+                        )
+                nc.scalar.copy(
+                    out=w_grouped[:, half * 2 * P : (half + 1) * 2 * P, :],
+                    in_=wt[:].rearrange("p t o -> p o t"),
+                )
+
+        def quantise_w():
+            nc.vector.quantize_mx(
+                out=w_codes[:].bitcast(FP8X4),
+                scales=w_scales[:],
+                in_=w_grouped[:].rearrange("p o t -> p (o t)"),
+            )
+
+        prods = {}
+        groupeds = {}
+        codes_of = {}
+        ostages = {}
+
+        def products(i):
+            if i in first_of_chunk:
+                tab = first_of_chunk[i]
+                nc.vector.tensor_scalar_mul(
+                    out=tab[:, 1, :, HH:H], in0=tab[:, 1, :, HH:H], scalar1=-1.0
+                )
+            xt, rl = x_of[i]
+            tab, tl = tab_of[i]
+            prod = prod_pool.tile([P, B, 2, H], F32, name="prod")
+            nc.vector.tensor_tensor(
+                out=prod[:],
+                in0=xt[:, :, rl, :].unsqueeze(2).to_broadcast([P, B, 2, H]),
+                in1=tab[:, :, tl, :].unsqueeze(1).to_broadcast([P, B, 2, H]),
+                op=MULT,
+            )
+            prods[i] = prod
+
+        def transposes_and_rounding(i):
+            prod = prods[i]
+            grouped = grp_pool.tile([P, B, P, KT], BF16, name="grouped", align_bytes=64)
+            for b in range(B):
+                h_t = psum_h.tile([P, KT, P], F32, name="h_t")
+                for t in range(KT):
+                    t2 = (t + KT // 2) % KT
+                    nc.tensor.matmul(
+                        out=h_t[:, t, :],
+                        lhsT=prod[:, b, 0, t * P : (t + 1) * P],
+                        rhs=ident_f[:],
+                        is_transpose=True,
+                        start=True,
+                        stop=False,
+                    )
+                    nc.tensor.matmul(
+                        out=h_t[:, t, :],
+                        lhsT=prod[:, b, 1, t2 * P : (t2 + 1) * P],
+                        rhs=ident_f[:],
+                        is_transpose=True,
+                        start=False,
+                        stop=True,
+                    )
+                nc.scalar.copy(out=grouped[:, b, :, :], in_=h_t[:].rearrange("p t l -> p l t"))
+            groupeds[i] = grouped
+
+        def quantise(i):
+            codes = code_pool.tile([P, B * P], U32, name="codes", align_bytes=64)
+            scales = code_pool.tile([P, B * P], U8, name="scales", align_bytes=64)
+            nc.vector.quantize_mx(
+                out=codes[:].bitcast(FP8X4),
+                scales=scales[:],
+                in_=groupeds[i][:].rearrange("p b l t -> p (b l t)"),
+            )
+            codes_of[i] = (codes, scales)
+
+        def project_and_store(i):
+            codes, scales = codes_of[i]
+            g = i // STORE_R
+            if i % STORE_R == 0:
+                ostages[g] = ost_pool.tile([P, B, STORE_R, H], F32, name="ostage")
+            ostage = ostages[g]
+            for b in range(B):
+                acc = psum_o.tile([P, H], F32, name="acc", tag="acc")
+                nc.tensor.matmul_mx(
+                    out=acc[:],
+                    lhsT=codes[:, b * P : (b + 1) * P].bitcast(FP8X4),
+                    lhsT_scale=scales[:, b * P : (b + 1) * P],
+                    rhs=w_codes[:].bitcast(FP8X4),
+                    rhs_scale=w_scales[:],
+                    start=True,
+                    stop=True,
+                )
+                nc.scalar.copy(out=ostage[:, b, i % STORE_R, :], in_=acc[:])
+            if i % STORE_R == STORE_R - 1:
+                nc.sync.dma_start(
+                    out=out_v[:, :, g * STORE_R : (g + 1) * STORE_R, :], in_=ostage[:]
+                )
+
+        prepare_w_transposes()
+        for i in range(R + 1):
+            if i < R:
+                products(i)
+                if i == 0:
+                    quantise_w()
+                transposes_and_rounding(i)
+            if i >= 1:
+                quantise(i - 1)
+                project_and_store(i - 1)

@@ -18,7 +18,8 @@ KT = H // P
 FLOPS = 2 * B * L * H * H + 3 * B * L * H
 
 LOAD_CHUNKS = [1, 1, 2, 4, 4, 4]
-STORE_R = 2
+UNITS = [(r, 0, B) for r in range(R - 1)] + [(R - 1, b, 1) for b in range(B)]
+LAG = 2
 
 
 def tile_denseattentiononehead_pa_t_kernel(tc, hidden_states, W_q, cos, sin, out):
@@ -32,9 +33,9 @@ def tile_denseattentiononehead_pa_t_kernel(tc, hidden_states, W_q, cos, sin, out
         const = ctx.enter_context(tc.tile_pool(name="const", bufs=1))
         resident = ctx.enter_context(tc.tile_pool(name="resident", bufs=1))
         prod_pool = ctx.enter_context(tc.tile_pool(name="prod", bufs=2))
-        grp_pool = ctx.enter_context(tc.tile_pool(name="grp", bufs=2))
+        grp_pool = ctx.enter_context(tc.tile_pool(name="grp", bufs=3))
         code_pool = ctx.enter_context(tc.tile_pool(name="code", bufs=2))
-        ost_pool = ctx.enter_context(tc.tile_pool(name="ost", bufs=3))
+        ost_pool = ctx.enter_context(tc.tile_pool(name="ost", bufs=4))
         psum_h = ctx.enter_context(tc.psum_pool(name="psum_h", bufs=4))
         psum_o = ctx.enter_context(tc.psum_pool(name="psum_o", bufs=4))
         ctx.enter_context(tc.manual_schedule())
@@ -93,35 +94,37 @@ def tile_denseattentiononehead_pa_t_kernel(tc, hidden_states, W_q, cos, sin, out
         prods = {}
         groupeds = {}
         codes_of = {}
-        ostages = {}
+        negated = set()
 
-        def products(i):
-            if i in first_of_chunk:
-                tab = first_of_chunk[i]
+        def products(u):
+            r, b0, nb = UNITS[u]
+            xt, rl = x_of[r]
+            tab, tl = tab_of[r]
+            if r in first_of_chunk and r not in negated:
+                negated.add(r)
                 nc.vector.tensor_scalar_mul(
                     out=tab[:, 1, :, HH:H], in0=tab[:, 1, :, HH:H], scalar1=-1.0
                 )
-            xt, rl = x_of[i]
-            tab, tl = tab_of[i]
             prod = prod_pool.tile([P, B, 2, H], F32, name="prod")
             nc.vector.tensor_tensor(
-                out=prod[:],
-                in0=xt[:, :, rl, :].unsqueeze(2).to_broadcast([P, B, 2, H]),
-                in1=tab[:, :, tl, :].unsqueeze(1).to_broadcast([P, B, 2, H]),
+                out=prod[:, 0:nb, :, :],
+                in0=xt[:, b0 : b0 + nb, rl, :].unsqueeze(2).to_broadcast([P, nb, 2, H]),
+                in1=tab[:, :, tl, :].unsqueeze(1).to_broadcast([P, nb, 2, H]),
                 op=MULT,
             )
-            prods[i] = prod
+            prods[u] = prod
 
-        def transposes_and_rounding(i):
-            prod = prods[i]
+        def transposes_and_rounding(u):
+            r, b0, nb = UNITS[u]
+            prod = prods[u]
             grouped = grp_pool.tile([P, B, P, KT], BF16, name="grouped", align_bytes=64)
-            for b in range(B):
+            for n in range(nb):
                 h_t = psum_h.tile([P, KT, P], F32, name="h_t")
                 for t in range(KT):
                     t2 = (t + KT // 2) % KT
                     nc.tensor.matmul(
                         out=h_t[:, t, :],
-                        lhsT=prod[:, b, 0, t * P : (t + 1) * P],
+                        lhsT=prod[:, n, 0, t * P : (t + 1) * P],
                         rhs=ident_f[:],
                         is_transpose=True,
                         start=True,
@@ -129,55 +132,51 @@ def tile_denseattentiononehead_pa_t_kernel(tc, hidden_states, W_q, cos, sin, out
                     )
                     nc.tensor.matmul(
                         out=h_t[:, t, :],
-                        lhsT=prod[:, b, 1, t2 * P : (t2 + 1) * P],
+                        lhsT=prod[:, n, 1, t2 * P : (t2 + 1) * P],
                         rhs=ident_f[:],
                         is_transpose=True,
                         start=False,
                         stop=True,
                     )
-                nc.scalar.copy(out=grouped[:, b, :, :], in_=h_t[:].rearrange("p t l -> p l t"))
-            groupeds[i] = grouped
+                nc.scalar.copy(out=grouped[:, n, :, :], in_=h_t[:].rearrange("p t l -> p l t"))
+            groupeds[u] = grouped
 
-        def quantise(i):
+        def quantise(u):
+            r, b0, nb = UNITS[u]
             codes = code_pool.tile([P, B * P], U32, name="codes", align_bytes=64)
             scales = code_pool.tile([P, B * P], U8, name="scales", align_bytes=64)
             nc.vector.quantize_mx(
-                out=codes[:].bitcast(FP8X4),
-                scales=scales[:],
-                in_=groupeds[i][:].rearrange("p b l t -> p (b l t)"),
+                out=codes[:, 0 : nb * P].bitcast(FP8X4),
+                scales=scales[:, 0 : nb * P],
+                in_=groupeds[u][:, 0:nb, :, :].rearrange("p b l t -> p (b l t)"),
             )
-            codes_of[i] = (codes, scales)
+            codes_of[u] = (codes, scales)
 
-        def project_and_store(i):
-            codes, scales = codes_of[i]
-            g = i // STORE_R
-            if i % STORE_R == 0:
-                ostages[g] = ost_pool.tile([P, B, STORE_R, H], F32, name="ostage")
-            ostage = ostages[g]
-            for b in range(B):
+        def project_and_store(u):
+            r, b0, nb = UNITS[u]
+            codes, scales = codes_of[u]
+            ostage = ost_pool.tile([P, B, H], F32, name="ostage")
+            for n in range(nb):
                 acc = psum_o.tile([P, H], F32, name="acc", tag="acc")
                 nc.tensor.matmul_mx(
                     out=acc[:],
-                    lhsT=codes[:, b * P : (b + 1) * P].bitcast(FP8X4),
-                    lhsT_scale=scales[:, b * P : (b + 1) * P],
+                    lhsT=codes[:, n * P : (n + 1) * P].bitcast(FP8X4),
+                    lhsT_scale=scales[:, n * P : (n + 1) * P],
                     rhs=w_codes[:].bitcast(FP8X4),
                     rhs_scale=w_scales[:],
                     start=True,
                     stop=True,
                 )
-                nc.scalar.copy(out=ostage[:, b, i % STORE_R, :], in_=acc[:])
-            if i % STORE_R == STORE_R - 1:
-                nc.sync.dma_start(
-                    out=out_v[:, :, g * STORE_R : (g + 1) * STORE_R, :], in_=ostage[:]
-                )
+                nc.scalar.copy(out=ostage[:, n, :], in_=acc[:])
+            nc.sync.dma_start(out=out_v[:, b0 : b0 + nb, r, :], in_=ostage[:, 0:nb, :])
 
         prepare_w_transposes()
-        for i in range(R + 1):
-            if i < R:
-                products(i)
-                if i == 0:
+        for u in range(len(UNITS) + LAG):
+            if u < len(UNITS):
+                products(u)
+                if u == 0:
                     quantise_w()
-                transposes_and_rounding(i)
-            if i >= 1:
-                quantise(i - 1)
-                project_and_store(i - 1)
+                transposes_and_rounding(u)
+            if u >= LAG:
+                quantise(u - LAG)
+                project_and_store(u - LAG)

@@ -20,6 +20,7 @@ FLOPS = 2 * B * L * H * H + 3 * B * L * H
 LOAD_CHUNKS = [1, 1, 2, 4, 4, 4]
 UNITS = [(r, 0, B) for r in range(R - 1)] + [(R - 1, b, 1) for b in range(B)]
 LAG = 2
+PAIR = 2
 
 
 def tile_denseattentiononehead_pa_t_kernel(tc, hidden_states, W_q, cos, sin, out):
@@ -94,6 +95,7 @@ def tile_denseattentiononehead_pa_t_kernel(tc, hidden_states, W_q, cos, sin, out
         prods = {}
         groupeds = {}
         codes_of = {}
+        ostages = {}
         negated = set()
 
         def products(u):
@@ -114,11 +116,13 @@ def tile_denseattentiononehead_pa_t_kernel(tc, hidden_states, W_q, cos, sin, out
             )
             prods[u] = prod
 
-        def transposes_and_rounding(u):
+        def transposes_and_rounding(u, n0):
             r, b0, nb = UNITS[u]
             prod = prods[u]
-            grouped = grp_pool.tile([P, B, P, KT], BF16, name="grouped", align_bytes=64)
-            for n in range(nb):
+            if n0 == 0:
+                groupeds[u] = grp_pool.tile([P, B, P, KT], BF16, name="grouped", align_bytes=64)
+            grouped = groupeds[u]
+            for n in range(n0, min(n0 + PAIR, nb)):
                 h_t = psum_h.tile([P, KT, P], F32, name="h_t")
                 for t in range(KT):
                     t2 = (t + KT // 2) % KT
@@ -139,7 +143,6 @@ def tile_denseattentiononehead_pa_t_kernel(tc, hidden_states, W_q, cos, sin, out
                         stop=True,
                     )
                 nc.scalar.copy(out=grouped[:, n, :, :], in_=h_t[:].rearrange("p t l -> p l t"))
-            groupeds[u] = grouped
 
         def quantise(u):
             r, b0, nb = UNITS[u]
@@ -152,11 +155,13 @@ def tile_denseattentiononehead_pa_t_kernel(tc, hidden_states, W_q, cos, sin, out
             )
             codes_of[u] = (codes, scales)
 
-        def project_and_store(u):
+        def project_and_store(u, n0):
             r, b0, nb = UNITS[u]
             codes, scales = codes_of[u]
-            ostage = ost_pool.tile([P, B, H], F32, name="ostage")
-            for n in range(nb):
+            if n0 == 0:
+                ostages[u] = ost_pool.tile([P, B, H], F32, name="ostage")
+            ostage = ostages[u]
+            for n in range(n0, min(n0 + PAIR, nb)):
                 acc = psum_o.tile([P, H], F32, name="acc", tag="acc")
                 nc.tensor.matmul_mx(
                     out=acc[:],
@@ -168,7 +173,8 @@ def tile_denseattentiononehead_pa_t_kernel(tc, hidden_states, W_q, cos, sin, out
                     stop=True,
                 )
                 nc.scalar.copy(out=ostage[:, n, :], in_=acc[:])
-            nc.sync.dma_start(out=out_v[:, b0 : b0 + nb, r, :], in_=ostage[:, 0:nb, :])
+            if n0 + PAIR >= nb and n0 < nb:
+                nc.sync.dma_start(out=out_v[:, b0 : b0 + nb, r, :], in_=ostage[:, 0:nb, :])
 
         prepare_w_transposes()
         for u in range(len(UNITS) + LAG):
@@ -176,7 +182,10 @@ def tile_denseattentiononehead_pa_t_kernel(tc, hidden_states, W_q, cos, sin, out
                 products(u)
                 if u == 0:
                     quantise_w()
-                transposes_and_rounding(u)
             if u >= LAG:
                 quantise(u - LAG)
-                project_and_store(u - LAG)
+            for n0 in range(0, B, PAIR):
+                if u < len(UNITS):
+                    transposes_and_rounding(u, n0)
+                if u >= LAG:
+                    project_and_store(u - LAG, n0)

@@ -18,8 +18,8 @@ KT = H // P
 FLOPS = 2 * B * L * H * H + 3 * B * L * H
 
 LOAD_CHUNKS = [1, 1, 2, 4, 4, 4]
-UNITS = [(r, 0, B) for r in range(R - 1)] + [(R - 1, b, 1) for b in range(B)]
-LAG = 2
+UNITS = [(r, 0, B) for r in range(R - 2)] + [(R - 2, 0, 2), (R - 2, 2, 2), (R - 1, 0, 2), (R - 1, 2, 1), (R - 1, 3, 1)]
+LAG = 1
 PAIR = 2
 
 
@@ -33,10 +33,10 @@ def tile_denseattentiononehead_pa_t_kernel(tc, hidden_states, W_q, cos, sin, out
     with ExitStack() as ctx:
         const = ctx.enter_context(tc.tile_pool(name="const", bufs=1))
         resident = ctx.enter_context(tc.tile_pool(name="resident", bufs=1))
-        prod_pool = ctx.enter_context(tc.tile_pool(name="prod", bufs=2))
+        prod_pool = ctx.enter_context(tc.tile_pool(name="prod", bufs=3))
         grp_pool = ctx.enter_context(tc.tile_pool(name="grp", bufs=3))
-        code_pool = ctx.enter_context(tc.tile_pool(name="code", bufs=2))
-        ost_pool = ctx.enter_context(tc.tile_pool(name="ost", bufs=4))
+        code_pool = ctx.enter_context(tc.tile_pool(name="code", bufs=3))
+        ost_pool = ctx.enter_context(tc.tile_pool(name="ost", bufs=5))
         psum_h = ctx.enter_context(tc.psum_pool(name="psum_h", bufs=4))
         psum_o = ctx.enter_context(tc.psum_pool(name="psum_o", bufs=4))
         ctx.enter_context(tc.manual_schedule())

@@ -18,8 +18,12 @@ KT = H // P
 FLOPS = 2 * B * L * H * H + 3 * B * L * H
 
 LOAD_CHUNKS = [1, 1, 2, 4, 4, 4]
-UNITS = [(r, 0, B) for r in range(R - 2)] + [(R - 2, 0, 2), (R - 2, 2, 2), (R - 1, 0, 2), (R - 1, 2, 1), (R - 1, 3, 1)]
-LAG = 1
+UNITS = (
+    [(0, 0, 2), (0, 2, 2)]
+    + [(r, 0, B) for r in range(1, R - 2)]
+    + [(R - 2, 0, 2), (R - 2, 2, 2), (R - 1, 0, 2), (R - 1, 2, 1), (R - 1, 3, 1)]
+)
+LAG = 2
 PAIR = 2
 
 
@@ -34,7 +38,7 @@ def tile_denseattentiononehead_pa_t_kernel(tc, hidden_states, W_q, cos, sin, out
         const = ctx.enter_context(tc.tile_pool(name="const", bufs=1))
         resident = ctx.enter_context(tc.tile_pool(name="resident", bufs=1))
         prod_pool = ctx.enter_context(tc.tile_pool(name="prod", bufs=3))
-        grp_pool = ctx.enter_context(tc.tile_pool(name="grp", bufs=3))
+        grp_pool = ctx.enter_context(tc.tile_pool(name="grp", bufs=4))
         code_pool = ctx.enter_context(tc.tile_pool(name="code", bufs=3))
         ost_pool = ctx.enter_context(tc.tile_pool(name="ost", bufs=5))
         psum_h = ctx.enter_context(tc.psum_pool(name="psum_h", bufs=4))
@@ -49,10 +53,11 @@ def tile_denseattentiononehead_pa_t_kernel(tc, hidden_states, W_q, cos, sin, out
         for c, rr in enumerate(LOAD_CHUNKS):
             xt = resident.tile([P, B, rr, H], BF16, name="x%d" % c)
             tab = resident.tile([P, 2, rr, H], BF16, name="tab%d" % c)
-            nc.sync.dma_start(out=xt[:], in_=x_v[:, :, r0 : r0 + rr, :])
             nc.sync.dma_start(out=tab[:, 0, :, :], in_=cos_v[:, r0 : r0 + rr, :])
             nc.sync.dma_start(out=tab[:, 1, :, 0:HH], in_=sin_v[:, r0 : r0 + rr, HH:H])
             nc.sync.dma_start(out=tab[:, 1, :, HH:H], in_=sin_v[:, r0 : r0 + rr, 0:HH])
+            for b0 in range(0, B, 2):
+                nc.sync.dma_start(out=xt[:, b0 : b0 + 2, :, :], in_=x_v[:, b0 : b0 + 2, r0 : r0 + rr, :])
             if c == 0:
                 nc.sync.dma_start(out=w_sb[:], in_=W_q.rearrange("(ob p) j -> p ob j", p=P))
             first_of_chunk[r0] = tab
@@ -180,8 +185,8 @@ def tile_denseattentiononehead_pa_t_kernel(tc, hidden_states, W_q, cos, sin, out
         for u in range(len(UNITS) + LAG):
             if u < len(UNITS):
                 products(u)
-                if u == 0:
-                    quantise_w()
+            if u == LAG:
+                quantise_w()
             if u >= LAG:
                 quantise(u - LAG)
             for n0 in range(0, B, PAIR):

@@ -24,6 +24,7 @@ UNITS = (
     + [(R - 2, 0, 2), (R - 2, 2, 2), (R - 1, 0, 2), (R - 1, 2, 1), (R - 1, 3, 1)]
 )
 LAG = 2
+GPSIMD_R = range(2, R - 2)
 PAIR = 2
 
 
@@ -38,11 +39,13 @@ def tile_denseattentiononehead_pa_t_kernel(tc, hidden_states, W_q, cos, sin, out
         const = ctx.enter_context(tc.tile_pool(name="const", bufs=1))
         resident = ctx.enter_context(tc.tile_pool(name="resident", bufs=1))
         prod_pool = ctx.enter_context(tc.tile_pool(name="prod", bufs=3))
+        gprod_pool = ctx.enter_context(tc.tile_pool(name="gprod", bufs=3))
         grp_pool = ctx.enter_context(tc.tile_pool(name="grp", bufs=4))
         code_pool = ctx.enter_context(tc.tile_pool(name="code", bufs=3))
         ost_pool = ctx.enter_context(tc.tile_pool(name="ost", bufs=5))
-        psum_h = ctx.enter_context(tc.psum_pool(name="psum_h", bufs=4))
-        psum_o = ctx.enter_context(tc.psum_pool(name="psum_o", bufs=4))
+        psum_h = ctx.enter_context(tc.psum_pool(name="psum_h", bufs=3))
+        psum_o = ctx.enter_context(tc.psum_pool(name="psum_o", bufs=3))
+        psum_t = ctx.enter_context(tc.psum_pool(name="psum_t", bufs=2))
         ctx.enter_context(tc.manual_schedule())
 
         x_of = {}
@@ -98,25 +101,48 @@ def tile_denseattentiononehead_pa_t_kernel(tc, hidden_states, W_q, cos, sin, out
             )
 
         prods = {}
+        gprods = {}
+        psum_tabs = {}
         groupeds = {}
         codes_of = {}
         ostages = {}
         negated = set()
 
+        def negate(r):
+            if r in first_of_chunk and r not in negated:
+                negated.add(r)
+                tab = first_of_chunk[r]
+                nc.vector.tensor_scalar_mul(
+                    out=tab[:, 1, :, HH:H], in0=tab[:, 1, :, HH:H], scalar1=-1.0
+                )
+
+        def tables_to_psum(r):
+            if r not in GPSIMD_R:
+                return
+            tab, tl = tab_of[r]
+            tab_p = psum_t.tile([P, 2, H], BF16, name="tab_p")
+            for i in range(2):
+                nc.tensor.matmul(out=tab_p[:, i, :], lhsT=ident_b[:], rhs=tab[:, i, tl, :], start=True, stop=True)
+            psum_tabs[r] = tab_p
+
         def products(u):
             r, b0, nb = UNITS[u]
             xt, rl = x_of[r]
             tab, tl = tab_of[r]
-            if r in first_of_chunk and r not in negated:
-                negated.add(r)
-                nc.vector.tensor_scalar_mul(
-                    out=tab[:, 1, :, HH:H], in0=tab[:, 1, :, HH:H], scalar1=-1.0
-                )
+            table = tab[:, :, tl, :]
             prod = prod_pool.tile([P, B, 2, H], F32, name="prod")
+            nv = nb
+            if r in GPSIMD_R:
+                nv = nb - 1
+                gprod = gprod_pool.tile([P, 2, H], F32, name="gprod")
+                for i in range(2):
+                    nc.gpsimd.tensor_tensor(out=gprod[:, i, :], in0=xt[:, nv, rl, :], in1=tab[:, i, tl, :], op=MULT)
+                gprods[u] = gprod
+                table = psum_tabs[r][:]
             nc.vector.tensor_tensor(
-                out=prod[:, 0:nb, :, :],
-                in0=xt[:, b0 : b0 + nb, rl, :].unsqueeze(2).to_broadcast([P, nb, 2, H]),
-                in1=tab[:, :, tl, :].unsqueeze(1).to_broadcast([P, nb, 2, H]),
+                out=prod[:, 0:nv, :, :],
+                in0=xt[:, b0 : b0 + nv, rl, :].unsqueeze(2).to_broadcast([P, nv, 2, H]),
+                in1=table.unsqueeze(1).to_broadcast([P, nv, 2, H]),
                 op=MULT,
             )
             prods[u] = prod
@@ -128,12 +154,13 @@ def tile_denseattentiononehead_pa_t_kernel(tc, hidden_states, W_q, cos, sin, out
                 groupeds[u] = grp_pool.tile([P, B, P, KT], BF16, name="grouped", align_bytes=64)
             grouped = groupeds[u]
             for n in range(n0, min(n0 + PAIR, nb)):
+                p_n = gprods[u] if u in gprods and n == nb - 1 else prod[:, n, :, :]
                 h_t = psum_h.tile([P, KT, P], F32, name="h_t")
                 for t in range(KT):
                     t2 = (t + KT // 2) % KT
                     nc.tensor.matmul(
                         out=h_t[:, t, :],
-                        lhsT=prod[:, n, 0, t * P : (t + 1) * P],
+                        lhsT=p_n[:, 0, t * P : (t + 1) * P],
                         rhs=ident_f[:],
                         is_transpose=True,
                         start=True,
@@ -141,7 +168,7 @@ def tile_denseattentiononehead_pa_t_kernel(tc, hidden_states, W_q, cos, sin, out
                     )
                     nc.tensor.matmul(
                         out=h_t[:, t, :],
-                        lhsT=prod[:, n, 1, t2 * P : (t2 + 1) * P],
+                        lhsT=p_n[:, 1, t2 * P : (t2 + 1) * P],
                         rhs=ident_f[:],
                         is_transpose=True,
                         start=False,
@@ -184,7 +211,12 @@ def tile_denseattentiononehead_pa_t_kernel(tc, hidden_states, W_q, cos, sin, out
         prepare_w_transposes()
         for u in range(len(UNITS) + LAG):
             if u < len(UNITS):
+                negate(UNITS[u][0])
                 products(u)
+            if u + 1 < len(UNITS):
+                negate(UNITS[u + 1][0])
+            if u + 2 < len(UNITS):
+                negate(UNITS[u + 2][0])
             if u == LAG:
                 quantise_w()
             if u >= LAG:
@@ -194,3 +226,5 @@ def tile_denseattentiononehead_pa_t_kernel(tc, hidden_states, W_q, cos, sin, out
                     transposes_and_rounding(u, n0)
                 if u >= LAG:
                     project_and_store(u - LAG, n0)
+            if u + 2 < len(UNITS):
+                tables_to_psum(UNITS[u + 2][0])

@@ -25,7 +25,7 @@ UNITS = (
 )
 LAG = 2
 GPSIMD_R = range(2, R - 2)
-PAIR = 2
+PAIR = 4
 
 
 def tile_denseattentiononehead_pa_t_kernel(tc, hidden_states, W_q, cos, sin, out):
@@ -43,8 +43,7 @@ def tile_denseattentiononehead_pa_t_kernel(tc, hidden_states, W_q, cos, sin, out
         grp_pool = ctx.enter_context(tc.tile_pool(name="grp", bufs=4))
         code_pool = ctx.enter_context(tc.tile_pool(name="code", bufs=3))
         ost_pool = ctx.enter_context(tc.tile_pool(name="ost", bufs=5))
-        psum_h = ctx.enter_context(tc.psum_pool(name="psum_h", bufs=3))
-        psum_o = ctx.enter_context(tc.psum_pool(name="psum_o", bufs=3))
+        psum_ho = ctx.enter_context(tc.psum_pool(name="psum_ho", bufs=6))
         psum_t = ctx.enter_context(tc.psum_pool(name="psum_t", bufs=2))
         ctx.enter_context(tc.manual_schedule())
 
@@ -80,7 +79,7 @@ def tile_denseattentiononehead_pa_t_kernel(tc, hidden_states, W_q, cos, sin, out
 
         def prepare_w_transposes():
             for half in range(2):
-                wt = psum_o.tile([P, KT, 2 * P], BF16, name="wt", tag="acc")
+                wt = psum_ho.tile([P, KT, 2 * P], BF16, name="wt", tag="bank")
                 for t in range(KT):
                     for o2 in range(2):
                         nc.tensor.transpose(
@@ -155,7 +154,7 @@ def tile_denseattentiononehead_pa_t_kernel(tc, hidden_states, W_q, cos, sin, out
             grouped = groupeds[u]
             for n in range(n0, min(n0 + PAIR, nb)):
                 p_n = gprods[u] if u in gprods and n == nb - 1 else prod[:, n, :, :]
-                h_t = psum_h.tile([P, KT, P], F32, name="h_t")
+                h_t = psum_ho.tile([P, KT, P], F32, name="h_t", tag="bank")
                 for t in range(KT):
                     t2 = (t + KT // 2) % KT
                     nc.tensor.matmul(
@@ -194,7 +193,7 @@ def tile_denseattentiononehead_pa_t_kernel(tc, hidden_states, W_q, cos, sin, out
                 ostages[u] = ost_pool.tile([P, B, H], F32, name="ostage")
             ostage = ostages[u]
             for n in range(n0, min(n0 + PAIR, nb)):
-                acc = psum_o.tile([P, H], F32, name="acc", tag="acc")
+                acc = psum_ho.tile([P, H], F32, name="acc", tag="bank")
                 nc.tensor.matmul_mx(
                     out=acc[:],
                     lhsT=codes[:, n * P : (n + 1) * P].bitcast(FP8X4),

@@ -17,14 +17,18 @@ R = L // P
 KT = H // P
 FLOPS = 2 * B * L * H * H + 3 * B * L * H
 
-LOAD_CHUNKS = [1, 1, 2, 4, 4, 4]
+LOAD_CHUNKS = [1, 1, 2, 2, 2, 4, 4]
 UNITS = (
     [(0, 0, 2), (0, 2, 2)]
     + [(r, 0, B) for r in range(1, R - 2)]
     + [(R - 2, 0, 2), (R - 2, 2, 2), (R - 1, 0, 2), (R - 1, 2, 1), (R - 1, 3, 1)]
 )
 LAG = 2
-GPSIMD_R = range(2, R - 2)
+GPSIMD_R = range(0, R)
+
+
+def v_sin(r):
+    return P
 PAIR = 4
 
 
@@ -39,10 +43,10 @@ def tile_denseattentiononehead_pa_t_kernel(tc, hidden_states, W_q, cos, sin, out
         const = ctx.enter_context(tc.tile_pool(name="const", bufs=1))
         resident = ctx.enter_context(tc.tile_pool(name="resident", bufs=1))
         prod_pool = ctx.enter_context(tc.tile_pool(name="prod", bufs=3))
-        gprod_pool = ctx.enter_context(tc.tile_pool(name="gprod", bufs=3))
+        gprod_pool = ctx.enter_context(tc.tile_pool(name="gprod", bufs=4))
         grp_pool = ctx.enter_context(tc.tile_pool(name="grp", bufs=4))
         code_pool = ctx.enter_context(tc.tile_pool(name="code", bufs=3))
-        ost_pool = ctx.enter_context(tc.tile_pool(name="ost", bufs=5))
+        ost_pool = ctx.enter_context(tc.tile_pool(name="ost", bufs=4))
         psum_ho = ctx.enter_context(tc.psum_pool(name="psum_ho", bufs=6))
         psum_t = ctx.enter_context(tc.psum_pool(name="psum_t", bufs=2))
         ctx.enter_context(tc.manual_schedule())
@@ -99,12 +103,15 @@ def tile_denseattentiononehead_pa_t_kernel(tc, hidden_states, W_q, cos, sin, out
                 in_=w_grouped[:].rearrange("p o t -> p (o t)"),
             )
 
-        prods = {}
-        gprods = {}
+        block_of = {}
         psum_tabs = {}
         groupeds = {}
         codes_of = {}
         ostages = {}
+        late_accs = {}
+
+        def v_copies(u):
+            return 1 if UNITS[u][2] == B else 0
         negated = set()
 
         def negate(r):
@@ -116,50 +123,52 @@ def tile_denseattentiononehead_pa_t_kernel(tc, hidden_states, W_q, cos, sin, out
                 )
 
         def tables_to_psum(r):
-            if r not in GPSIMD_R:
+            if r not in GPSIMD_R or r in psum_tabs:
                 return
             tab, tl = tab_of[r]
-            tab_p = psum_t.tile([P, 2, H], BF16, name="tab_p")
-            for i in range(2):
-                nc.tensor.matmul(out=tab_p[:, i, :], lhsT=ident_b[:], rhs=tab[:, i, tl, :], start=True, stop=True)
+            tab_p = psum_t.tile([P, H + v_sin(r)], BF16, name="tab_p")
+            nc.tensor.matmul(out=tab_p[:, 0:H], lhsT=ident_b[:], rhs=tab[:, 0, tl, :], start=True, stop=True)
+            nc.tensor.matmul(out=tab_p[:, H : H + v_sin(r)], lhsT=ident_b[:], rhs=tab[:, 1, tl, 0:v_sin(r)], start=True, stop=True)
             psum_tabs[r] = tab_p
 
         def products(u):
             r, b0, nb = UNITS[u]
             xt, rl = x_of[r]
             tab, tl = tab_of[r]
-            table = tab[:, :, tl, :]
-            prod = prod_pool.tile([P, B, 2, H], F32, name="prod")
-            nv = nb
-            if r in GPSIMD_R:
-                nv = nb - 1
-                gprod = gprod_pool.tile([P, 2, H], F32, name="gprod")
-                for i in range(2):
-                    nc.gpsimd.tensor_tensor(out=gprod[:, i, :], in0=xt[:, nv, rl, :], in1=tab[:, i, tl, :], op=MULT)
-                gprods[u] = gprod
-                table = psum_tabs[r][:]
-            nc.vector.tensor_tensor(
-                out=prod[:, 0:nv, :, :],
-                in0=xt[:, b0 : b0 + nv, rl, :].unsqueeze(2).to_broadcast([P, nv, 2, H]),
-                in1=table.unsqueeze(1).to_broadcast([P, nv, 2, H]),
-                op=MULT,
-            )
-            prods[u] = prod
+            x = xt[:, b0 : b0 + nb, rl, :]
+            gprod = gprod_pool.tile([P, B, H - v_sin(r)], F32, name="gprod")
+            for n in range(nb):
+                nc.gpsimd.tensor_tensor(out=gprod[:, n, :], in0=x[:, n, v_sin(r):H], in1=tab[:, 1, tl, v_sin(r):H], op=MULT)
+            prod = prod_pool.tile([P, B, H + v_sin(r)], F32, name="vprod", tag="vprod")
+            tab_p = psum_tabs[r]
+            for c0, c1 in ((0, H), (H, H + v_sin(r))):
+                nc.vector.tensor_tensor(
+                    out=prod[:, 0:nb, c0:c1],
+                    in0=x[:, :, 0 : c1 - c0],
+                    in1=tab_p[:, c0:c1].unsqueeze(1).to_broadcast([P, nb, c1 - c0]),
+                    op=MULT,
+                )
+
+            def block(n, i, t):
+                if i == 1 and t * P >= v_sin(r):
+                    return gprod[:, n, t * P - v_sin(r) : (t + 1) * P - v_sin(r)]
+                return prod[:, n, i * H + t * P : i * H + (t + 1) * P]
+
+            block_of[u] = block
 
         def transposes_and_rounding(u, n0):
             r, b0, nb = UNITS[u]
-            prod = prods[u]
+            block = block_of[u]
             if n0 == 0:
                 groupeds[u] = grp_pool.tile([P, B, P, KT], BF16, name="grouped", align_bytes=64)
             grouped = groupeds[u]
             for n in range(n0, min(n0 + PAIR, nb)):
-                p_n = gprods[u] if u in gprods and n == nb - 1 else prod[:, n, :, :]
                 h_t = psum_ho.tile([P, KT, P], F32, name="h_t", tag="bank")
                 for t in range(KT):
                     t2 = (t + KT // 2) % KT
                     nc.tensor.matmul(
                         out=h_t[:, t, :],
-                        lhsT=p_n[:, 0, t * P : (t + 1) * P],
+                        lhsT=block(n, 0, t),
                         rhs=ident_f[:],
                         is_transpose=True,
                         start=True,
@@ -167,7 +176,7 @@ def tile_denseattentiononehead_pa_t_kernel(tc, hidden_states, W_q, cos, sin, out
                     )
                     nc.tensor.matmul(
                         out=h_t[:, t, :],
-                        lhsT=p_n[:, 1, t2 * P : (t2 + 1) * P],
+                        lhsT=block(n, 1, t2),
                         rhs=ident_f[:],
                         is_transpose=True,
                         start=False,
@@ -203,27 +212,41 @@ def tile_denseattentiononehead_pa_t_kernel(tc, hidden_states, W_q, cos, sin, out
                     start=True,
                     stop=True,
                 )
-                nc.scalar.copy(out=ostage[:, n, :], in_=acc[:])
-            if n0 + PAIR >= nb and n0 < nb:
-                nc.sync.dma_start(out=out_v[:, b0 : b0 + nb, r, :], in_=ostage[:, 0:nb, :])
+                if n >= nb - v_copies(u):
+                    late_accs.setdefault(u, []).append((n, acc))
+                else:
+                    nc.scalar.copy(out=ostage[:, n, :], in_=acc[:])
+            if u not in late_accs:
+                store(u)
 
+        def store(u):
+            r, b0, nb = UNITS[u]
+            nc.sync.dma_start(out=out_v[:, b0 : b0 + nb, r, :], in_=ostages[u][:, 0:nb, :])
+
+        def finish(u):
+            if u in late_accs:
+                for n, acc in late_accs[u]:
+                    nc.vector.tensor_copy(out=ostages[u][:, n, :], in_=acc[:])
+                store(u)
+
+        negate(0)
+        tables_to_psum(0)
         prepare_w_transposes()
-        for u in range(len(UNITS) + LAG):
+        for u in range(len(UNITS) + LAG + 1):
             if u < len(UNITS):
-                negate(UNITS[u][0])
                 products(u)
-            if u + 1 < len(UNITS):
-                negate(UNITS[u + 1][0])
-            if u + 2 < len(UNITS):
-                negate(UNITS[u + 2][0])
             if u == LAG:
                 quantise_w()
-            if u >= LAG:
+            if LAG <= u < len(UNITS) + LAG:
                 quantise(u - LAG)
+            if u > LAG:
+                finish(u - LAG - 1)
+            if u + 2 < len(UNITS):
+                negate(UNITS[u + 2][0])
             for n0 in range(0, B, PAIR):
                 if u < len(UNITS):
                     transposes_and_rounding(u, n0)
-                if u >= LAG:
+                if LAG <= u < len(UNITS) + LAG:
                     project_and_store(u - LAG, n0)
             if u + 2 < len(UNITS):
                 tables_to_psum(UNITS[u + 2][0])

@@ -24,11 +24,7 @@ UNITS = (
     + [(R - 2, 0, 2), (R - 2, 2, 2), (R - 1, 0, 2), (R - 1, 2, 1), (R - 1, 3, 1)]
 )
 LAG = 2
-GPSIMD_R = range(0, R)
 
-
-def v_sin(r):
-    return P
 PAIR = 4
 
 
@@ -53,7 +49,6 @@ def tile_denseattentiononehead_pa_t_kernel(tc, hidden_states, W_q, cos, sin, out
 
         x_of = {}
         tab_of = {}
-        first_of_chunk = {}
         w_sb = const.tile([P, KT, H], BF16, name="w_sb")
         r0 = 0
         for c, rr in enumerate(LOAD_CHUNKS):
@@ -66,7 +61,6 @@ def tile_denseattentiononehead_pa_t_kernel(tc, hidden_states, W_q, cos, sin, out
                 nc.sync.dma_start(out=xt[:, b0 : b0 + 2, :, :], in_=x_v[:, b0 : b0 + 2, r0 : r0 + rr, :])
             if c == 0:
                 nc.sync.dma_start(out=w_sb[:], in_=W_q.rearrange("(ob p) j -> p ob j", p=P))
-            first_of_chunk[r0] = tab
             for rl in range(rr):
                 x_of[r0 + rl] = (xt, rl)
                 tab_of[r0 + rl] = (tab, rl)
@@ -111,24 +105,23 @@ def tile_denseattentiononehead_pa_t_kernel(tc, hidden_states, W_q, cos, sin, out
         late_accs = {}
 
         def v_copies(u):
-            return 1 if UNITS[u][2] == B else 0
+            return UNITS[u][0] % 2 if UNITS[u][2] == B else 0
         negated = set()
 
         def negate(r):
-            if r in first_of_chunk and r not in negated:
-                negated.add(r)
-                tab = first_of_chunk[r]
-                nc.vector.tensor_scalar_mul(
-                    out=tab[:, 1, :, HH:H], in0=tab[:, 1, :, HH:H], scalar1=-1.0
-                )
+            if r in negated:
+                return
+            negated.add(r)
+            tab, tl = tab_of[r]
+            nc.vector.tensor_scalar_mul(out=tab[:, 1, tl, HH:H], in0=tab[:, 1, tl, HH:H], scalar1=-1.0)
 
         def tables_to_psum(r):
-            if r not in GPSIMD_R or r in psum_tabs:
+            if r in psum_tabs:
                 return
             tab, tl = tab_of[r]
-            tab_p = psum_t.tile([P, H + v_sin(r)], BF16, name="tab_p")
+            tab_p = psum_t.tile([P, H + HH], BF16, name="tab_p")
             nc.tensor.matmul(out=tab_p[:, 0:H], lhsT=ident_b[:], rhs=tab[:, 0, tl, :], start=True, stop=True)
-            nc.tensor.matmul(out=tab_p[:, H : H + v_sin(r)], lhsT=ident_b[:], rhs=tab[:, 1, tl, 0:v_sin(r)], start=True, stop=True)
+            nc.tensor.matmul(out=tab_p[:, H : H + HH], lhsT=ident_b[:], rhs=tab[:, 1, tl, 0:HH], start=True, stop=True)
             psum_tabs[r] = tab_p
 
         def products(u):
@@ -136,12 +129,17 @@ def tile_denseattentiononehead_pa_t_kernel(tc, hidden_states, W_q, cos, sin, out
             xt, rl = x_of[r]
             tab, tl = tab_of[r]
             x = xt[:, b0 : b0 + nb, rl, :]
-            gprod = gprod_pool.tile([P, B, H - v_sin(r)], F32, name="gprod")
-            for n in range(nb):
-                nc.gpsimd.tensor_tensor(out=gprod[:, n, :], in0=x[:, n, v_sin(r):H], in1=tab[:, 1, tl, v_sin(r):H], op=MULT)
-            prod = prod_pool.tile([P, B, H + v_sin(r)], F32, name="vprod", tag="vprod")
+            negate(r)
+            gprod = gprod_pool.tile([P, B, H - HH], F32, name="gprod")
+            nc.gpsimd.tensor_tensor(
+                out=gprod[:, 0:nb, :],
+                in0=x[:, :, HH:H],
+                in1=tab[:, 1, tl, HH:H].unsqueeze(1).to_broadcast([P, nb, HH]),
+                op=MULT,
+            )
+            prod = prod_pool.tile([P, B, H + HH], F32, name="vprod", tag="vprod")
             tab_p = psum_tabs[r]
-            for c0, c1 in ((0, H), (H, H + v_sin(r))):
+            for c0, c1 in ((0, H), (H, H + HH)):
                 nc.vector.tensor_tensor(
                     out=prod[:, 0:nb, c0:c1],
                     in0=x[:, :, 0 : c1 - c0],
@@ -150,8 +148,8 @@ def tile_denseattentiononehead_pa_t_kernel(tc, hidden_states, W_q, cos, sin, out
                 )
 
             def block(n, i, t):
-                if i == 1 and t * P >= v_sin(r):
-                    return gprod[:, n, t * P - v_sin(r) : (t + 1) * P - v_sin(r)]
+                if i == 1 and t * P >= HH:
+                    return gprod[:, n, t * P - HH : (t + 1) * P - HH]
                 return prod[:, n, i * H + t * P : i * H + (t + 1) * P]
 
             block_of[u] = block
@@ -229,9 +227,9 @@ def tile_denseattentiononehead_pa_t_kernel(tc, hidden_states, W_q, cos, sin, out
                     nc.vector.tensor_copy(out=ostages[u][:, n, :], in_=acc[:])
                 store(u)
 
-        negate(0)
         tables_to_psum(0)
         prepare_w_transposes()
+        tables_to_psum(1)
         for u in range(len(UNITS) + LAG + 1):
             if u < len(UNITS):
                 products(u)
@@ -241,8 +239,6 @@ def tile_denseattentiononehead_pa_t_kernel(tc, hidden_states, W_q, cos, sin, out
                 quantise(u - LAG)
             if u > LAG:
                 finish(u - LAG - 1)
-            if u + 2 < len(UNITS):
-                negate(UNITS[u + 2][0])
             for n0 in range(0, B, PAIR):
                 if u < len(UNITS):
                     transposes_and_rounding(u, n0)

@@ -17,7 +17,9 @@ R = L // P
 KT = H // P
 FLOPS = 2 * B * L * H * H + 3 * B * L * H
 
-LOAD_CHUNKS = [1, 1, 2, 2, 2, 4, 4]
+LOAD_CHUNKS = [1, 1, 2, 2, 2, 2, 2, 2, 2]
+EARLY_CHUNKS = 5
+AHEAD = 5
 UNITS = (
     [(0, 0, 2), (0, 2, 2)]
     + [(r, 0, B) for r in range(1, R - 2)]
@@ -42,7 +44,7 @@ def tile_denseattentiononehead_pa_t_kernel(tc, hidden_states, W_q, cos, sin, out
         gprod_pool = ctx.enter_context(tc.tile_pool(name="gprod", bufs=4))
         grp_pool = ctx.enter_context(tc.tile_pool(name="grp", bufs=4))
         code_pool = ctx.enter_context(tc.tile_pool(name="code", bufs=3))
-        ost_pool = ctx.enter_context(tc.tile_pool(name="ost", bufs=4))
+        ost_pool = ctx.enter_context(tc.tile_pool(name="ost", bufs=6))
         psum_ho = ctx.enter_context(tc.psum_pool(name="psum_ho", bufs=6))
         psum_t = ctx.enter_context(tc.psum_pool(name="psum_t", bufs=2))
         ctx.enter_context(tc.manual_schedule())
@@ -50,21 +52,24 @@ def tile_denseattentiononehead_pa_t_kernel(tc, hidden_states, W_q, cos, sin, out
         x_of = {}
         tab_of = {}
         w_sb = const.tile([P, KT, H], BF16, name="w_sb")
-        r0 = 0
-        for c, rr in enumerate(LOAD_CHUNKS):
+        chunk_r0 = [sum(LOAD_CHUNKS[:c]) for c in range(len(LOAD_CHUNKS))]
+
+        def load_chunk(c):
+            r0, rr = chunk_r0[c], LOAD_CHUNKS[c]
             xt = resident.tile([P, B, rr, H], BF16, name="x%d" % c)
             tab = resident.tile([P, 2, rr, H], BF16, name="tab%d" % c)
             nc.sync.dma_start(out=tab[:, 0, :, :], in_=cos_v[:, r0 : r0 + rr, :])
-            nc.sync.dma_start(out=tab[:, 1, :, 0:HH], in_=sin_v[:, r0 : r0 + rr, HH:H])
-            nc.sync.dma_start(out=tab[:, 1, :, HH:H], in_=sin_v[:, r0 : r0 + rr, 0:HH])
+            nc.sync.dma_start(out=tab[:, 1, :, :], in_=sin_v[:, r0 : r0 + rr, :])
             for b0 in range(0, B, 2):
                 nc.sync.dma_start(out=xt[:, b0 : b0 + 2, :, :], in_=x_v[:, b0 : b0 + 2, r0 : r0 + rr, :])
-            if c == 0:
-                nc.sync.dma_start(out=w_sb[:], in_=W_q.rearrange("(ob p) j -> p ob j", p=P))
             for rl in range(rr):
                 x_of[r0 + rl] = (xt, rl)
                 tab_of[r0 + rl] = (tab, rl)
-            r0 += rr
+
+        load_chunk(0)
+        nc.sync.dma_start(out=w_sb[:], in_=W_q.rearrange("(ob p) j -> p ob j", p=P))
+        for c in range(1, EARLY_CHUNKS):
+            load_chunk(c)
 
         ident_f = const.tile([P, P], F32, name="ident_f")
         make_identity(nc, ident_f[:])
@@ -113,7 +118,7 @@ def tile_denseattentiononehead_pa_t_kernel(tc, hidden_states, W_q, cos, sin, out
                 return
             negated.add(r)
             tab, tl = tab_of[r]
-            nc.vector.tensor_scalar_mul(out=tab[:, 1, tl, HH:H], in0=tab[:, 1, tl, HH:H], scalar1=-1.0)
+            nc.vector.tensor_scalar_mul(out=tab[:, 1, tl, 0:HH], in0=tab[:, 1, tl, 0:HH], scalar1=-1.0)
 
         def tables_to_psum(r):
             if r in psum_tabs:
@@ -121,7 +126,7 @@ def tile_denseattentiononehead_pa_t_kernel(tc, hidden_states, W_q, cos, sin, out
             tab, tl = tab_of[r]
             tab_p = psum_t.tile([P, H + HH], BF16, name="tab_p")
             nc.tensor.matmul(out=tab_p[:, 0:H], lhsT=ident_b[:], rhs=tab[:, 0, tl, :], start=True, stop=True)
-            nc.tensor.matmul(out=tab_p[:, H : H + HH], lhsT=ident_b[:], rhs=tab[:, 1, tl, 0:HH], start=True, stop=True)
+            nc.tensor.matmul(out=tab_p[:, H : H + HH], lhsT=ident_b[:], rhs=tab[:, 1, tl, HH:H], start=True, stop=True)
             psum_tabs[r] = tab_p
 
         def products(u):
@@ -134,7 +139,7 @@ def tile_denseattentiononehead_pa_t_kernel(tc, hidden_states, W_q, cos, sin, out
             nc.gpsimd.tensor_tensor(
                 out=gprod[:, 0:nb, :],
                 in0=x[:, :, HH:H],
-                in1=tab[:, 1, tl, HH:H].unsqueeze(1).to_broadcast([P, nb, HH]),
+                in1=tab[:, 1, tl, 0:HH].unsqueeze(1).to_broadcast([P, nb, HH]),
                 op=MULT,
             )
             prod = prod_pool.tile([P, B, H + HH], F32, name="vprod", tag="vprod")
@@ -230,6 +235,7 @@ def tile_denseattentiononehead_pa_t_kernel(tc, hidden_states, W_q, cos, sin, out
         tables_to_psum(0)
         prepare_w_transposes()
         tables_to_psum(1)
+        loaded = EARLY_CHUNKS
         for u in range(len(UNITS) + LAG + 1):
             if u < len(UNITS):
                 products(u)
@@ -246,3 +252,6 @@ def tile_denseattentiononehead_pa_t_kernel(tc, hidden_states, W_q, cos, sin, out
                     project_and_store(u - LAG, n0)
             if u + 2 < len(UNITS):
                 tables_to_psum(UNITS[u + 2][0])
+            if u < len(UNITS) and loaded < len(LOAD_CHUNKS) and UNITS[u][0] + AHEAD >= chunk_r0[loaded]:
+                load_chunk(loaded)
+                loaded += 1

@@ -26,6 +26,7 @@ UNITS = (
     + [(R - 2, 0, 2), (R - 2, 2, 2), (R - 1, 0, 2), (R - 1, 2, 1), (R - 1, 3, 1)]
 )
 LAG = 2
+VECTOR_COPIES_FROM = 11
 
 PAIR = 4
 
@@ -110,7 +111,7 @@ def tile_denseattentiononehead_pa_t_kernel(tc, hidden_states, W_q, cos, sin, out
         late_accs = {}
 
         def v_copies(u):
-            return UNITS[u][0] % 2 if UNITS[u][2] == B else 0
+            return 1 if UNITS[u][2] > 1 and UNITS[u][0] >= VECTOR_COPIES_FROM else 0
         negated = set()
 
         def negate(r):

from contextlib import ExitStack

import concourse.mybir as mybir
from concourse.masks import make_identity

FP8X4 = mybir.dt.float8_e4m3fn_x4
BF16 = mybir.dt.bfloat16
F32 = mybir.dt.float32
U32 = mybir.dt.uint32
U8 = mybir.dt.uint8
MULT = mybir.AluOpType.mult

B, L, H = 4, 2048, 512
HH = H // 2
P = 128
R = L // P
KT = H // P
FLOPS = 2 * B * L * H * H + 3 * B * L * H

LOAD_CHUNKS = [1, 1, 2, 2, 2, 2, 2, 2, 2]
EARLY_CHUNKS = 5
AHEAD = 5
UNITS = (
    [(0, 0, 2), (0, 2, 2)]
    + [(r, 0, B) for r in range(1, R - 2)]
    + [(R - 2, 0, 2), (R - 2, 2, 2), (R - 1, 0, 2), (R - 1, 2, 1), (R - 1, 3, 1)]
)
LAG = 2
VECTOR_COPIES_FROM = 11

PAIR = 4


def tile_denseattentiononehead_pa_t_kernel(tc, hidden_states, W_q, cos, sin, out):
    nc = tc.nc
    x_v = hidden_states.rearrange("b (p r) j -> p b r j", r=R)
    cos_v = cos.rearrange("(p r) j -> p r j", r=R)
    sin_v = sin.rearrange("(p r) j -> p r j", r=R)
    out_v = out.rearrange("b (p r) o -> p b r o", r=R)

    with ExitStack() as ctx:
        const = ctx.enter_context(tc.tile_pool(name="const", bufs=1))
        resident = ctx.enter_context(tc.tile_pool(name="resident", bufs=1))
        prod_pool = ctx.enter_context(tc.tile_pool(name="prod", bufs=3))
        gprod_pool = ctx.enter_context(tc.tile_pool(name="gprod", bufs=4))
        grp_pool = ctx.enter_context(tc.tile_pool(name="grp", bufs=4))
        code_pool = ctx.enter_context(tc.tile_pool(name="code", bufs=3))
        ost_pool = ctx.enter_context(tc.tile_pool(name="ost", bufs=6))
        psum_ho = ctx.enter_context(tc.psum_pool(name="psum_ho", bufs=6))
        psum_t = ctx.enter_context(tc.psum_pool(name="psum_t", bufs=2))
        ctx.enter_context(tc.manual_schedule())

        x_of = {}
        tab_of = {}
        w_sb = const.tile([P, KT, H], BF16, name="w_sb")
        chunk_r0 = [sum(LOAD_CHUNKS[:c]) for c in range(len(LOAD_CHUNKS))]

        def load_chunk(c):
            r0, rr = chunk_r0[c], LOAD_CHUNKS[c]
            xt = resident.tile([P, B, rr, H], BF16, name="x%d" % c)
            tab = resident.tile([P, 2, rr, H], BF16, name="tab%d" % c)
            nc.sync.dma_start(out=tab[:, 0, :, :], in_=cos_v[:, r0 : r0 + rr, :])
            nc.sync.dma_start(out=tab[:, 1, :, :], in_=sin_v[:, r0 : r0 + rr, :])
            for b0 in range(0, B, 2):
                nc.sync.dma_start(out=xt[:, b0 : b0 + 2, :, :], in_=x_v[:, b0 : b0 + 2, r0 : r0 + rr, :])
            for rl in range(rr):
                x_of[r0 + rl] = (xt, rl)
                tab_of[r0 + rl] = (tab, rl)

        load_chunk(0)
        nc.sync.dma_start(out=w_sb[:], in_=W_q.rearrange("(ob p) j -> p ob j", p=P))
        for c in range(1, EARLY_CHUNKS):
            load_chunk(c)

        ident_f = const.tile([P, P], F32, name="ident_f")
        make_identity(nc, ident_f[:])
        ident_b = const.tile([P, P], BF16, name="ident_b")
        make_identity(nc, ident_b[:])

        w_grouped = const.tile([P, H, KT], BF16, name="w_grouped", align_bytes=64)
        w_codes = const.tile([P, H], U32, name="w_codes", align_bytes=64)
        w_scales = const.tile([P, H], U8, name="w_scales", align_bytes=64)

        def prepare_w_transposes():
            for half in range(2):
                wt = psum_ho.tile([P, KT, 2 * P], BF16, name="wt", tag="bank")
                for t in range(KT):
                    for o2 in range(2):
                        nc.tensor.transpose(
                            wt[:, t, o2 * P : (o2 + 1) * P],
                            w_sb[:, 2 * half + o2, t * P : (t + 1) * P],
                            ident_b[:],
                        )
                nc.scalar.copy(
                    out=w_grouped[:, half * 2 * P : (half + 1) * 2 * P, :],
                    in_=wt[:].rearrange("p t o -> p o t"),
                )

        def quantise_w():
            nc.vector.quantize_mx(
                out=w_codes[:].bitcast(FP8X4),
                scales=w_scales[:],
                in_=w_grouped[:].rearrange("p o t -> p (o t)"),
            )

        block_of = {}
        psum_tabs = {}
        groupeds = {}
        codes_of = {}
        ostages = {}
        late_accs = {}

        def v_copies(u):
            return 1 if UNITS[u][2] > 1 and UNITS[u][0] >= VECTOR_COPIES_FROM else 0
        negated = set()

        def negate(r):
            if r in negated:
                return
            negated.add(r)
            tab, tl = tab_of[r]
            nc.vector.tensor_scalar_mul(out=tab[:, 1, tl, 0:HH], in0=tab[:, 1, tl, 0:HH], scalar1=-1.0)

        def tables_to_psum(r):
            if r in psum_tabs:
                return
            tab, tl = tab_of[r]
            tab_p = psum_t.tile([P, H + HH], BF16, name="tab_p")
            nc.tensor.matmul(out=tab_p[:, 0:H], lhsT=ident_b[:], rhs=tab[:, 0, tl, :], start=True, stop=True)
            nc.tensor.matmul(out=tab_p[:, H : H + HH], lhsT=ident_b[:], rhs=tab[:, 1, tl, HH:H], start=True, stop=True)
            psum_tabs[r] = tab_p

        def products(u):
            r, b0, nb = UNITS[u]
            xt, rl = x_of[r]
            tab, tl = tab_of[r]
            x = xt[:, b0 : b0 + nb, rl, :]
            negate(r)
            gprod = gprod_pool.tile([P, B, H - HH], F32, name="gprod")
            nc.gpsimd.tensor_tensor(
                out=gprod[:, 0:nb, :],
                in0=x[:, :, HH:H],
                in1=tab[:, 1, tl, 0:HH].unsqueeze(1).to_broadcast([P, nb, HH]),
                op=MULT,
            )
            prod = prod_pool.tile([P, B, H + HH], F32, name="vprod", tag="vprod")
            tab_p = psum_tabs[r]
            for c0, c1 in ((0, H), (H, H + HH)):
                nc.vector.tensor_tensor(
                    out=prod[:, 0:nb, c0:c1],
                    in0=x[:, :, 0 : c1 - c0],
                    in1=tab_p[:, c0:c1].unsqueeze(1).to_broadcast([P, nb, c1 - c0]),
                    op=MULT,
                )

            def block(n, i, t):
                if i == 1 and t * P >= HH:
                    return gprod[:, n, t * P - HH : (t + 1) * P - HH]
                return prod[:, n, i * H + t * P : i * H + (t + 1) * P]

            block_of[u] = block

        def transposes_and_rounding(u, n0):
            r, b0, nb = UNITS[u]
            block = block_of[u]
            if n0 == 0:
                groupeds[u] = grp_pool.tile([P, B, P, KT], BF16, name="grouped", align_bytes=64)
            grouped = groupeds[u]
            for n in range(n0, min(n0 + PAIR, nb)):
                h_t = psum_ho.tile([P, KT, P], F32, name="h_t", tag="bank")
                for t in range(KT):
                    t2 = (t + KT // 2) % KT
                    nc.tensor.matmul(
                        out=h_t[:, t, :],
                        lhsT=block(n, 0, t),
                        rhs=ident_f[:],
                        is_transpose=True,
                        start=True,
                        stop=False,
                    )
                    nc.tensor.matmul(
                        out=h_t[:, t, :],
                        lhsT=block(n, 1, t2),
                        rhs=ident_f[:],
                        is_transpose=True,
                        start=False,
                        stop=True,
                    )
                nc.scalar.copy(out=grouped[:, n, :, :], in_=h_t[:].rearrange("p t l -> p l t"))

        def quantise(u):
            r, b0, nb = UNITS[u]
            codes = code_pool.tile([P, B * P], U32, name="codes", align_bytes=64)
            scales = code_pool.tile([P, B * P], U8, name="scales", align_bytes=64)
            nc.vector.quantize_mx(
                out=codes[:, 0 : nb * P].bitcast(FP8X4),
                scales=scales[:, 0 : nb * P],
                in_=groupeds[u][:, 0:nb, :, :].rearrange("p b l t -> p (b l t)"),
            )
            codes_of[u] = (codes, scales)

        def project_and_store(u, n0):
            r, b0, nb = UNITS[u]
            codes, scales = codes_of[u]
            if n0 == 0:
                ostages[u] = ost_pool.tile([P, B, H], F32, name="ostage")
            ostage = ostages[u]
            for n in range(n0, min(n0 + PAIR, nb)):
                acc = psum_ho.tile([P, H], F32, name="acc", tag="bank")
                nc.tensor.matmul_mx(
                    out=acc[:],
                    lhsT=codes[:, n * P : (n + 1) * P].bitcast(FP8X4),
                    lhsT_scale=scales[:, n * P : (n + 1) * P],
                    rhs=w_codes[:].bitcast(FP8X4),
                    rhs_scale=w_scales[:],
                    start=True,
                    stop=True,
                )
                if n >= nb - v_copies(u):
                    late_accs.setdefault(u, []).append((n, acc))
                else:
                    nc.scalar.copy(out=ostage[:, n, :], in_=acc[:])
            if u not in late_accs:
                store(u)

        def store(u):
            r, b0, nb = UNITS[u]
            nc.sync.dma_start(out=out_v[:, b0 : b0 + nb, r, :], in_=ostages[u][:, 0:nb, :])

        def finish(u):
            if u in late_accs:
                for n, acc in late_accs[u]:
                    nc.vector.tensor_copy(out=ostages[u][:, n, :], in_=acc[:])
                store(u)

        tables_to_psum(0)
        prepare_w_transposes()
        tables_to_psum(1)
        loaded = EARLY_CHUNKS
        for u in range(len(UNITS) + LAG + 1):
            if u < len(UNITS):
                products(u)
            if u == LAG:
                quantise_w()
            if LAG <= u < len(UNITS) + LAG:
                quantise(u - LAG)
            if u > LAG:
                finish(u - LAG - 1)
            for n0 in range(0, B, PAIR):
                if u < len(UNITS):
                    transposes_and_rounding(u, n0)
                if LAG <= u < len(UNITS) + LAG:
                    project_and_store(u - LAG, n0)
            if u + 2 < len(UNITS):
                tables_to_psum(UNITS[u + 2][0])
            if u < len(UNITS) and loaded < len(LOAD_CHUNKS) and UNITS[u][0] + AHEAD >= chunk_r0[loaded]:
                load_chunk(loaded)
                loaded += 1
